import numpy as np
import ml_dtypes


def mxq(x, axis, fmt="e4m3"):
    dtype, down = {"e4m3": (ml_dtypes.float8_e4m3fn, 7), "e5m2": (ml_dtypes.float8_e5m2, 14)}[fmt]
    v = np.moveaxis(np.asarray(x, np.float32).astype(ml_dtypes.bfloat16).astype(np.float64), axis, -1)
    blocks = v.reshape(v.shape[:-1] + (-1, 32))
    amax = np.abs(blocks).max(-1, keepdims=True)
    byte = np.maximum(np.where(amax > 0, np.frexp(amax)[1] - 1 + 127, 0) - down, 1)
    scale = np.exp2(byte - 127.0)
    codes = (blocks / scale).astype(np.float32).astype(dtype).astype(np.float64)
    return np.moveaxis((codes * scale).reshape(v.shape), -1, axis)


WIDE = False


def mx_kscale(k):
    if not WIDE:
        return np.ones(k)
    levels = np.array([10, -10, 5, -5, 0])
    a = np.random.permutation(np.resize(levels, k // 512 * 4)).reshape(k // 512, 4)
    idx = np.arange(k)
    return np.exp2(a[idx // 512, idx % 128 // 32])


BF16 = ml_dtypes.bfloat16


def bf(x):
    return np.asarray(x, np.float32).astype(BF16)


def f64(x):
    return np.asarray(x).astype(np.float64)


E2M1 = np.array([0.0, 0.5, 1.0, 1.5, 2.0, 3.0, 4.0, 6.0, -0.0, -0.5, -1.0, -1.5, -2.0, -3.0, -4.0, -6.0])


def pack_weight(w, fmt):
    k, n = w.shape
    w = f64(bf(w)).reshape(k // 32, 32, n)
    amax = np.abs(w).max(1)
    if fmt == "e4m3":
        byte = np.frexp(amax)[1] - 1 + 127 - 7
    else:
        mant, ex = np.frexp(amax / 6.0)
        byte = np.where(mant > 0.5, ex, ex - 1) + 127
    byte = np.clip(np.where(amax > 0, byte, 1), 1, 254)
    scaled = (w * np.exp2(127.0 - byte)[:, None, :]).reshape(k, n).astype(np.float32)
    by_word = np.ascontiguousarray(scaled.reshape(k // 512, 128, 4, n).transpose(0, 1, 3, 2))
    if fmt == "e4m3":
        words = by_word.astype(ml_dtypes.float8_e4m3fn).view(np.uint8)
    else:
        c = by_word.astype(ml_dtypes.float4_e2m1fn).view(np.uint8) & 0xF
        words = c[..., 0::2] | (c[..., 1::2] << 4)
    return np.ascontiguousarray(words), np.ascontiguousarray(byte.astype(np.uint8).reshape(k // 512, 16, n))


def unpack_weight(words, scales, fmt):
    g, p, n, _ = words.shape
    if fmt == "e4m3":
        vals = np.ascontiguousarray(words).view(ml_dtypes.float8_e4m3fn).astype(np.float64)
    else:
        nib = np.empty((g, p, n, 4), np.uint8)
        nib[..., 0::2] = words & 0xF
        nib[..., 1::2] = words >> 4
        vals = E2M1[nib]
    vals = vals * np.repeat(np.exp2(scales.astype(np.float64) - 127.0), 8, axis=1)[..., None]
    return vals.transpose(0, 1, 3, 2).reshape(g * 512, n)


B, IN_F, OUT_F = 128, 8192, 2560
EPS = 1e-5


def setup_inputs():
    s = mx_kscale(IN_F)
    scale = 1.0 / np.sqrt(IN_F)
    x = bf(np.random.standard_normal((B, IN_F)) * s)
    y = bf(np.random.standard_normal((B, OUT_F)))
    weight = np.random.uniform(-scale, scale, (OUT_F, IN_F)) / s[None, :]
    weight_words, weight_scales = pack_weight(np.ascontiguousarray(weight.T), "e4m3")
    return {"x": x,
            "y": y,
            "weight_words": weight_words,
            "weight_scales": weight_scales,
            "bias": bf(np.random.uniform(-0.5, 0.5, OUT_F)),
            "running_mean": bf(np.random.standard_normal(OUT_F) * 0.3),
            "running_var": bf(np.random.uniform(0.5, 1.5, OUT_F)),
            "norm_weight": bf(1.0 + 0.1 * np.random.standard_normal(OUT_F)),
            "norm_bias": bf(np.random.standard_normal(OUT_F) * 0.3)}


def reference(x, y, weight_words, weight_scales, bias, running_mean, running_var, norm_weight, norm_bias):
    linear = (mxq(f64(x), 1, "e4m3") @ unpack_weight(weight_words, weight_scales, "e4m3")) + f64(bias)
    inv_std = 1.0 / np.sqrt(f64(running_var) + EPS)
    norm = (linear - f64(running_mean)) * inv_std * f64(norm_weight) + f64(norm_bias)
    return (norm + f64(y)) * f64(y)

@@ -1,0 +1,199 @@
+from contextlib import ExitStack
+
+import concourse.mybir as mybir
+from concourse.masks import make_identity
+
+FP8X4 = mybir.dt.float8_e4m3fn_x4
+BF16 = mybir.dt.bfloat16
+F32 = mybir.dt.float32
+I32 = mybir.dt.int32
+U32 = mybir.dt.uint32
+U8 = mybir.dt.uint8
+ALU = mybir.AluOpType
+ACT = mybir.ActivationFunctionType
+
+P = 128
+K = 8192
+N = 2560
+GROUPS = K // 512
+NT = 512
+TILES = N // NT
+EPS = 1e-5
+FLOPS = 2 * P * K * N
+
+SCALES_ON_GPSIMD = False
+TAIL_GROUPS = 3
+W_BUFS = 8
+
+
+def tile_modelnew_w_kernel(
+    tc, x, y, weight_words, weight_scales, bias, running_mean, running_var, norm_weight, norm_bias, out
+):
+    nc = tc.nc
+    head_groups = GROUPS - TAIL_GROUPS
+    ww = weight_words.rearrange("g p n t -> g p (n t)").bitcast(I32)
+
+    with ExitStack() as ctx:
+        keep = ctx.enter_context(tc.tile_pool(name="keep", bufs=1))
+        wpool = ctx.enter_context(tc.tile_pool(name="wstream", bufs=W_BUFS))
+        opool = ctx.enter_context(tc.tile_pool(name="outs", bufs=3))
+        accp = ctx.enter_context(tc.psum_pool(name="accp", bufs=1))
+        tpp = ctx.enter_context(tc.psum_pool(name="tpp", bufs=3))
+        ctx.enter_context(tc.manual_schedule())
+
+        x_sb = []
+        for c in range(4):
+            xt = keep.tile([P, 2048], BF16, name="x%d" % c)
+            nc.sync.dma_start(out=xt[:], in_=x[:, 2048 * c : 2048 * (c + 1)])
+            x_sb.append(xt)
+
+        ident = keep.tile([P, P], F32, name="ident")
+        make_identity(nc, ident[:])
+
+        planes = []
+        for gq in range(4):
+            pl = keep.tile([P, N], U8, name="pl%d" % gq, align_bytes=64)
+            nc.vector.memset(pl[:].bitcast(I32), 0)
+            planes.append(pl)
+        vecs = keep.tile([P, P], BF16, name="vecs")
+        nc.vector.memset(vecs[:], 0.0)
+
+        for v, vec_ap in enumerate((bias, running_mean, running_var, norm_weight, norm_bias)):
+            nc.scalar.dma_start(out=vecs[20 * v : 20 * v + 20, :], in_=vec_ap.rearrange("(c j) -> c j", j=P))
+
+        for gq in range(4):
+            for q in range(4):
+                dst = planes[gq][32 * q : 32 * q + 16, :]
+                src = weight_scales[4 * gq : 4 * gq + 4, 4 * q : 4 * q + 4, :]
+                if SCALES_ON_GPSIMD:
+                    nc.gpsimd.dma_start(out=dst.bitcast(F32), in_=src.bitcast(F32))
+                else:
+                    nc.sync.dma_start(out=dst.bitcast(I32), in_=src.bitcast(I32))
+
+        w_sb = {}
+
+        def load_w(g):
+            wt = wpool.tile([P, N], U32, name="w", tag="w", align_bytes=64)
+            nc.sync.dma_start(out=wt[:].bitcast(I32), in_=ww[g])
+            w_sb[g] = wt
+
+        y_sb = keep.tile([P, N], BF16, name="y_sb")
+        load_w(0)
+        nc.sync.dma_start(out=y_sb[:], in_=y)
+        for g in range(1, W_BUFS):
+            load_w(g)
+
+        xc = []
+        xs = []
+        grps = []
+
+        def quantise(rd):
+            nc.vector.quantize_mx(
+                out=xc[rd][:].bitcast(FP8X4),
+                scales=xs[rd][:],
+                in_=grps[rd][:].rearrange("p g b t -> p (g b t)"),
+            )
+
+        for rd in range(8):
+            x32 = x_sb[rd // 2][:].bitcast(F32)
+            tp = tpp.tile([P, 2, 2, P], F32, name="tp", tag="tp")
+            for g2 in range(2):
+                base = 256 * ((2 * rd + g2) % 4)
+                for u in range(2):
+                    nc.tensor.transpose(tp[:, g2, u, :], x32[:, base + u : base + 256 : 2], ident[:])
+            grp = keep.tile([P, 2, P, 4], BF16, name="grp%d" % rd, align_bytes=64)
+            nc.scalar.copy(out=grp[:].bitcast(F32), in_=tp[:].rearrange("p g u b -> p g b u"))
+            grps.append(grp)
+            xc.append(keep.tile([P, 2 * P], U32, name="xc%d" % rd, align_bytes=64))
+            xs.append(keep.tile([P, 2 * P], U8, name="xs%d" % rd, align_bytes=64))
+            if rd >= 1:
+                quantise(rd - 1)
+        quantise(7)
+
+        vecs32 = keep.tile([P, P], F32, name="vecs32")
+        nc.vector.tensor_copy(out=vecs32[:], in_=vecs[:])
+        tv = tpp.tile([P, 2, 2, P], F32, name="tv", tag="tp")
+        nc.tensor.transpose(tv[:, 0, 0, :], vecs32[:], ident[:])
+        vt = keep.tile([P, P], F32, name="vt")
+        nc.vector.tensor_copy(out=vt[:], in_=tv[:, 0, 0, :])
+        ab = keep.tile([P, 40], F32, name="ab")
+        tmp = keep.tile([P, 40], F32, name="tmp")
+        nc.vector.tensor_scalar_add(out=tmp[:, 0:20], in0=vt[:, 40:60], scalar1=EPS)
+        nc.scalar.sqrt(out=tmp[:, 0:20], in_=tmp[:, 0:20])
+        nc.vector.reciprocal(out=tmp[:, 0:20], in_=tmp[:, 0:20])
+        nc.vector.tensor_tensor(out=ab[:, 0:20], in0=tmp[:, 0:20], in1=vt[:, 60:80], op=ALU.mult)
+        nc.vector.tensor_tensor(out=tmp[:, 20:40], in0=vt[:, 0:20], in1=vt[:, 20:40], op=ALU.subtract)
+        nc.vector.tensor_tensor(out=tmp[:, 20:40], in0=tmp[:, 20:40], in1=ab[:, 0:20], op=ALU.mult)
+        nc.vector.tensor_tensor(out=ab[:, 20:40], in0=tmp[:, 20:40], in1=vt[:, 80:100], op=ALU.add)
+
+        pm = []
+        qm = []
+
+        def spread(t):
+            cols = slice(NT * t, NT * (t + 1))
+            ba = tpp.tile([P, 4, P], F32, name="ba", tag="tp")
+            bb = tpp.tile([P, 4, P], F32, name="bb", tag="tp")
+            for i in range(4):
+                c = 4 * t + i
+                nc.tensor.transpose(ba[:, i, :], ab[:, c : c + 1].to_broadcast([P, P]), ident[:])
+            for i in range(4):
+                c = 20 + 4 * t + i
+                nc.tensor.transpose(bb[:, i, :], ab[:, c : c + 1].to_broadcast([P, P]), ident[:])
+            pt = keep.tile([P, NT], F32, name="pm%d" % t)
+            qt = keep.tile([P, NT], F32, name="qm%d" % t)
+            nc.vector.tensor_tensor(out=pt[:], in0=ba[:].rearrange("p i j -> p (i j)"), in1=y_sb[:, cols], op=ALU.mult)
+            nc.vector.tensor_tensor(out=qt[:], in0=bb[:].rearrange("p i j -> p (i j)"), in1=y_sb[:, cols], op=ALU.add)
+            nc.vector.tensor_tensor(out=qt[:], in0=qt[:], in1=y_sb[:, cols], op=ALU.mult)
+            pm.append(pt)
+            qm.append(qt)
+
+        acc = [accp.tile([P, NT], F32, name="acc%d" % j) for j in range(TILES)]
+
+        def mx_pass(g, j, words):
+            rd, g2 = divmod(g, 2)
+            gq, kq = divmod(g, 4)
+            nc.tensor.matmul_mx(
+                out=acc[j][:],
+                lhsT=xc[rd][:, P * g2 : P * (g2 + 1)].bitcast(FP8X4),
+                lhsT_scale=xs[rd][:, P * g2 : P * (g2 + 1)],
+                rhs=words.bitcast(FP8X4),
+                rhs_scale=planes[gq][4 * kq : P, NT * j : NT * (j + 1)],
+                start=(g == 0),
+                stop=(g == GROUPS - 1),
+            )
+
+        tail_w = {}
+
+        def load_tail():
+            for j in range(TILES):
+                cols = slice(NT * j, NT * (j + 1))
+                if j < TILES - 1:
+                    wt = keep.tile([P, TAIL_GROUPS, NT], U32, name="wt%d" % j, align_bytes=64)
+                    nc.sync.dma_start(out=wt[:].bitcast(I32), in_=ww[head_groups:GROUPS, :, cols].rearrange("g p n -> p g n"))
+                    for i in range(TAIL_GROUPS):
+                        tail_w[(head_groups + i, j)] = wt[:, i, :]
+                else:
+                    for i in range(TAIL_GROUPS):
+                        wl = keep.tile([P, NT], U32, name="wl%d" % i, align_bytes=64)
+                        nc.sync.dma_start(out=wl[:].bitcast(I32), in_=ww[head_groups + i, :, cols])
+                        tail_w[(head_groups + i, j)] = wl[:]
+
+        for g in range(head_groups):
+            for j in range(TILES):
+                mx_pass(g, j, w_sb[g][:, NT * j : NT * (j + 1)])
+            nxt = g + W_BUFS
+            if nxt < head_groups:
+                load_w(nxt)
+            elif nxt == head_groups:
+                load_tail()
+            if 1 <= g <= TILES:
+                spread(g - 1)
+
+        for j in range(TILES):
+            cols = slice(NT * j, NT * (j + 1))
+            for g in range(head_groups, GROUPS):
+                mx_pass(g, j, tail_w[(g, j)])
+            o = opool.tile([P, NT], F32, name="o", tag="o")
+            nc.vector.tensor_tensor(out=o[:], in0=acc[j][:], in1=pm[j][:], op=ALU.mult)
+            nc.vector.tensor_tensor(out=o[:], in0=o[:], in1=qm[j][:], op=ALU.add)
+            nc.sync.dma_start(out=out[:, cols], in_=o[:])

@@ -21,7 +21,7 @@ TILES = N // NT
 EPS = 1e-5
 FLOPS = 2 * P * K * N
 
-SCALES_ON_GPSIMD = False
+SCALES_ON_GPSIMD = True
 TAIL_GROUPS = 3
 W_BUFS = 8
 

@@ -24,6 +24,8 @@ FLOPS = 2 * P * K * N
 SCALES_ON_GPSIMD = True
 TAIL_GROUPS = 3
 W_BUFS = 8
+X_CHUNKS = 2
+LAST_WIDTHS = (256, 128, 128)
 
 
 def tile_modelnew_w_kernel(
@@ -42,9 +44,10 @@ def tile_modelnew_w_kernel(
         ctx.enter_context(tc.manual_schedule())
 
         x_sb = []
-        for c in range(4):
-            xt = keep.tile([P, 2048], BF16, name="x%d" % c)
-            nc.sync.dma_start(out=xt[:], in_=x[:, 2048 * c : 2048 * (c + 1)])
+        xw = K // X_CHUNKS
+        for c in range(X_CHUNKS):
+            xt = keep.tile([P, xw], BF16, name="x%d" % c)
+            nc.sync.dma_start(out=xt[:], in_=x[:, xw * c : xw * (c + 1)])
             x_sb.append(xt)
 
         ident = keep.tile([P, P], F32, name="ident")
@@ -95,10 +98,11 @@ def tile_modelnew_w_kernel(
             )
 
         for rd in range(8):
-            x32 = x_sb[rd // 2][:].bitcast(F32)
+            per = 8 // X_CHUNKS
+            x32 = x_sb[rd // per][:].bitcast(F32)
             tp = tpp.tile([P, 2, 2, P], F32, name="tp", tag="tp")
             for g2 in range(2):
-                base = 256 * ((2 * rd + g2) % 4)
+                base = 256 * ((2 * rd + g2) % (2 * per))
                 for u in range(2):
                     nc.tensor.transpose(tp[:, g2, u, :], x32[:, base + u : base + 256 : 2], ident[:])
             grp = keep.tile([P, 2, P, 4], BF16, name="grp%d" % rd, align_bytes=64)
@@ -149,38 +153,49 @@ def tile_modelnew_w_kernel(
 
         acc = [accp.tile([P, NT], F32, name="acc%d" % j) for j in range(TILES)]
 
-        def mx_pass(g, j, words):
+        def mx_pass(g, dst, col0, width, words, start, stop):
             rd, g2 = divmod(g, 2)
             gq, kq = divmod(g, 4)
             nc.tensor.matmul_mx(
-                out=acc[j][:],
+                out=dst,
                 lhsT=xc[rd][:, P * g2 : P * (g2 + 1)].bitcast(FP8X4),
                 lhsT_scale=xs[rd][:, P * g2 : P * (g2 + 1)],
                 rhs=words.bitcast(FP8X4),
-                rhs_scale=planes[gq][4 * kq : P, NT * j : NT * (j + 1)],
-                start=(g == 0),
-                stop=(g == GROUPS - 1),
+                rhs_scale=planes[gq][4 * kq : P, col0 : col0 + width],
+                start=start,
+                stop=stop,
             )
 
         tail_w = {}
+        last = TILES - 1
+        pieces = []
+        col = NT * last
+        for width in LAST_WIDTHS:
+            pieces.append((col, width))
+            col += width
 
         def load_tail():
-            for j in range(TILES):
-                cols = slice(NT * j, NT * (j + 1))
-                if j < TILES - 1:
-                    wt = keep.tile([P, TAIL_GROUPS, NT], U32, name="wt%d" % j, align_bytes=64)
-                    nc.sync.dma_start(out=wt[:].bitcast(I32), in_=ww[head_groups:GROUPS, :, cols].rearrange("g p n -> p g n"))
-                    for i in range(TAIL_GROUPS):
-                        tail_w[(head_groups + i, j)] = wt[:, i, :]
-                else:
-                    for i in range(TAIL_GROUPS):
-                        wl = keep.tile([P, NT], U32, name="wl%d" % i, align_bytes=64)
-                        nc.sync.dma_start(out=wl[:].bitcast(I32), in_=ww[head_groups + i, :, cols])
-                        tail_w[(head_groups + i, j)] = wl[:]
+            for j in range(last):
+                wt = keep.tile([P, TAIL_GROUPS, NT], U32, name="wt%d" % j, align_bytes=64)
+                nc.sync.dma_start(
+                    out=wt[:].bitcast(I32),
+                    in_=ww[head_groups:GROUPS, :, NT * j : NT * (j + 1)].rearrange("g p n -> p g n"),
+                )
+                tail_w[j] = wt
+            for s, (col0, width) in enumerate(pieces):
+                wl = keep.tile([P, TAIL_GROUPS, width], U32, name="wl%d" % s, align_bytes=64)
+                nc.sync.dma_start(
+                    out=wl[:].bitcast(I32),
+                    in_=ww[head_groups:GROUPS, :, col0 : col0 + width].rearrange("g p n -> p g n"),
+                )
+                tail_w[(last, s)] = wl
 
         for g in range(head_groups):
             for j in range(TILES):
-                mx_pass(g, j, w_sb[g][:, NT * j : NT * (j + 1)])
+                mx_pass(
+                    g, acc[j][:], NT * j, NT, w_sb[g][:, NT * j : NT * (j + 1)],
+                    g == 0, j == last and g == head_groups - 1,
+                )
             nxt = g + W_BUFS
             if nxt < head_groups:
                 load_w(nxt)
@@ -189,11 +204,24 @@ def tile_modelnew_w_kernel(
             if 1 <= g <= TILES:
                 spread(g - 1)
 
-        for j in range(TILES):
-            cols = slice(NT * j, NT * (j + 1))
-            for g in range(head_groups, GROUPS):
-                mx_pass(g, j, tail_w[(g, j)])
+        rest = keep.tile([P, NT], F32, name="rest")
+        nc.vector.tensor_tensor(out=rest[:], in0=acc[last][:], in1=pm[last][:], op=ALU.mult)
+        nc.vector.tensor_tensor(out=rest[:], in0=rest[:], in1=qm[last][:], op=ALU.add)
+
+        for j in range(last):
+            for i in range(TAIL_GROUPS):
+                mx_pass(head_groups + i, acc[j][:], NT * j, NT, tail_w[j][:, i, :], False, i == TAIL_GROUPS - 1)
             o = opool.tile([P, NT], F32, name="o", tag="o")
             nc.vector.tensor_tensor(out=o[:], in0=acc[j][:], in1=pm[j][:], op=ALU.mult)
             nc.vector.tensor_tensor(out=o[:], in0=o[:], in1=qm[j][:], op=ALU.add)
-            nc.sync.dma_start(out=out[:, cols], in_=o[:])
+            nc.sync.dma_start(out=out[:, NT * j : NT * (j + 1)], in_=o[:])
+
+        for s, (col0, width) in enumerate(pieces):
+            lo = col0 - NT * last
+            part = tpp.tile([P, NT], F32, name="part", tag="tp")
+            for i in range(TAIL_GROUPS):
+                mx_pass(head_groups + i, part[:, 0:width], col0, width, tail_w[(last, s)][:, i, :], i == 0, i == TAIL_GROUPS - 1)
+            ol = opool.tile([P, NT], F32, name="ol", tag="o")
+            nc.vector.tensor_tensor(out=ol[:, 0:width], in0=part[:, 0:width], in1=pm[last][:, lo : lo + width], op=ALU.mult)
+            nc.vector.tensor_tensor(out=ol[:, 0:width], in0=ol[:, 0:width], in1=rest[:, lo : lo + width], op=ALU.add)
+            nc.sync.dma_start(out=out[:, col0 : col0 + width], in_=ol[:, 0:width])

@@ -38,7 +38,7 @@ def tile_modelnew_w_kernel(
     with ExitStack() as ctx:
         keep = ctx.enter_context(tc.tile_pool(name="keep", bufs=1))
         wpool = ctx.enter_context(tc.tile_pool(name="wstream", bufs=W_BUFS))
-        opool = ctx.enter_context(tc.tile_pool(name="outs", bufs=3))
+        opool = ctx.enter_context(tc.tile_pool(name="outs", bufs=7))
         accp = ctx.enter_context(tc.psum_pool(name="accp", bufs=1))
         tpp = ctx.enter_context(tc.psum_pool(name="tpp", bufs=3))
         ctx.enter_context(tc.manual_schedule())

@@ -25,7 +25,6 @@ SCALES_ON_GPSIMD = True
 TAIL_GROUPS = 3
 W_BUFS = 8
 X_CHUNKS = 2
-LAST_WIDTHS = (256, 128, 128)
 
 
 def tile_modelnew_w_kernel(
@@ -38,7 +37,7 @@ def tile_modelnew_w_kernel(
     with ExitStack() as ctx:
         keep = ctx.enter_context(tc.tile_pool(name="keep", bufs=1))
         wpool = ctx.enter_context(tc.tile_pool(name="wstream", bufs=W_BUFS))
-        opool = ctx.enter_context(tc.tile_pool(name="outs", bufs=7))
+        opool = ctx.enter_context(tc.tile_pool(name="outs", bufs=5))
         accp = ctx.enter_context(tc.psum_pool(name="accp", bufs=1))
         tpp = ctx.enter_context(tc.psum_pool(name="tpp", bufs=3))
         ctx.enter_context(tc.manual_schedule())
@@ -65,7 +64,7 @@ def tile_modelnew_w_kernel(
             nc.scalar.dma_start(out=vecs[20 * v : 20 * v + 20, :], in_=vec_ap.rearrange("(c j) -> c j", j=P))
 
         for gq in range(4):
-            for q in range(4):
+            for q in (0, 2, 1, 3):
                 dst = planes[gq][32 * q : 32 * q + 16, :]
                 src = weight_scales[4 * gq : 4 * gq + 4, 4 * q : 4 * q + 4, :]
                 if SCALES_ON_GPSIMD:
@@ -153,49 +152,46 @@ def tile_modelnew_w_kernel(
 
         acc = [accp.tile([P, NT], F32, name="acc%d" % j) for j in range(TILES)]
 
-        def mx_pass(g, dst, col0, width, words, start, stop):
+        def mx_pass(g, j, words):
             rd, g2 = divmod(g, 2)
             gq, kq = divmod(g, 4)
             nc.tensor.matmul_mx(
-                out=dst,
+                out=acc[j][:],
                 lhsT=xc[rd][:, P * g2 : P * (g2 + 1)].bitcast(FP8X4),
                 lhsT_scale=xs[rd][:, P * g2 : P * (g2 + 1)],
                 rhs=words.bitcast(FP8X4),
-                rhs_scale=planes[gq][4 * kq : P, col0 : col0 + width],
-                start=start,
-                stop=stop,
+                rhs_scale=planes[gq][4 * kq : P, NT * j : NT * (j + 1)],
+                start=(g == 0),
+                stop=(g == GROUPS - 1),
             )
 
         tail_w = {}
-        last = TILES - 1
-        pieces = []
-        col = NT * last
-        for width in LAST_WIDTHS:
-            pieces.append((col, width))
-            col += width
 
         def load_tail():
-            for j in range(last):
-                wt = keep.tile([P, TAIL_GROUPS, NT], U32, name="wt%d" % j, align_bytes=64)
-                nc.sync.dma_start(
-                    out=wt[:].bitcast(I32),
-                    in_=ww[head_groups:GROUPS, :, NT * j : NT * (j + 1)].rearrange("g p n -> p g n"),
-                )
-                tail_w[j] = wt
-            for s, (col0, width) in enumerate(pieces):
-                wl = keep.tile([P, TAIL_GROUPS, width], U32, name="wl%d" % s, align_bytes=64)
-                nc.sync.dma_start(
-                    out=wl[:].bitcast(I32),
-                    in_=ww[head_groups:GROUPS, :, col0 : col0 + width].rearrange("g p n -> p g n"),
-                )
-                tail_w[(last, s)] = wl
+            for j in range(TILES):
+                cols = slice(NT * j, NT * (j + 1))
+                if j == 0:
+                    wt = keep.tile([P, TAIL_GROUPS, 2 * NT], U32, name="wt01", align_bytes=64)
+                    nc.sync.dma_start(out=wt[:].bitcast(I32), in_=ww[head_groups:GROUPS, :, 0 : 2 * NT].rearrange("g p n -> p g n"))
+                    for i in range(TAIL_GROUPS):
+                        tail_w[(head_groups + i, 0)] = wt[:, i, 0:NT]
+                        tail_w[(head_groups + i, 1)] = wt[:, i, NT : 2 * NT]
+                elif j == 1:
+                    continue
+                elif j < TILES - 1:
+                    wt = keep.tile([P, TAIL_GROUPS, NT], U32, name="wt%d" % j, align_bytes=64)
+                    nc.sync.dma_start(out=wt[:].bitcast(I32), in_=ww[head_groups:GROUPS, :, cols].rearrange("g p n -> p g n"))
+                    for i in range(TAIL_GROUPS):
+                        tail_w[(head_groups + i, j)] = wt[:, i, :]
+                else:
+                    for i in range(TAIL_GROUPS):
+                        wl = keep.tile([P, NT], U32, name="wl%d" % i, align_bytes=64)
+                        nc.sync.dma_start(out=wl[:].bitcast(I32), in_=ww[head_groups + i, :, cols])
+                        tail_w[(head_groups + i, j)] = wl[:]
 
         for g in range(head_groups):
             for j in range(TILES):
-                mx_pass(
-                    g, acc[j][:], NT * j, NT, w_sb[g][:, NT * j : NT * (j + 1)],
-                    g == 0, j == last and g == head_groups - 1,
-                )
+                mx_pass(g, j, w_sb[g][:, NT * j : NT * (j + 1)])
             nxt = g + W_BUFS
             if nxt < head_groups:
                 load_w(nxt)
@@ -204,24 +200,11 @@ def tile_modelnew_w_kernel(
             if 1 <= g <= TILES:
                 spread(g - 1)
 
-        rest = keep.tile([P, NT], F32, name="rest")
-        nc.vector.tensor_tensor(out=rest[:], in0=acc[last][:], in1=pm[last][:], op=ALU.mult)
-        nc.vector.tensor_tensor(out=rest[:], in0=rest[:], in1=qm[last][:], op=ALU.add)
-
-        for j in range(last):
-            for i in range(TAIL_GROUPS):
-                mx_pass(head_groups + i, acc[j][:], NT * j, NT, tail_w[j][:, i, :], False, i == TAIL_GROUPS - 1)
+        for j in range(TILES):
+            cols = slice(NT * j, NT * (j + 1))
+            for g in range(head_groups, GROUPS):
+                mx_pass(g, j, tail_w[(g, j)])
             o = opool.tile([P, NT], F32, name="o", tag="o")
             nc.vector.tensor_tensor(out=o[:], in0=acc[j][:], in1=pm[j][:], op=ALU.mult)
             nc.vector.tensor_tensor(out=o[:], in0=o[:], in1=qm[j][:], op=ALU.add)
-            nc.sync.dma_start(out=out[:, NT * j : NT * (j + 1)], in_=o[:])
-
-        for s, (col0, width) in enumerate(pieces):
-            lo = col0 - NT * last
-            part = tpp.tile([P, NT], F32, name="part", tag="tp")
-            for i in range(TAIL_GROUPS):
-                mx_pass(head_groups + i, part[:, 0:width], col0, width, tail_w[(last, s)][:, i, :], i == 0, i == TAIL_GROUPS - 1)
-            ol = opool.tile([P, NT], F32, name="ol", tag="o")
-            nc.vector.tensor_tensor(out=ol[:, 0:width], in0=part[:, 0:width], in1=pm[last][:, lo : lo + width], op=ALU.mult)
-            nc.vector.tensor_tensor(out=ol[:, 0:width], in0=ol[:, 0:width], in1=rest[:, lo : lo + width], op=ALU.add)
-            nc.sync.dma_start(out=out[:, col0 : col0 + width], in_=ol[:, 0:width])
+            nc.sync.dma_start(out=out[:, cols], in_=o[:])

@@ -64,7 +64,7 @@ def tile_modelnew_w_kernel(
             nc.scalar.dma_start(out=vecs[20 * v : 20 * v + 20, :], in_=vec_ap.rearrange("(c j) -> c j", j=P))
 
         for gq in range(4):
-            for q in (0, 2, 1, 3):
+            for q in range(4):
                 dst = planes[gq][32 * q : 32 * q + 16, :]
                 src = weight_scales[4 * gq : 4 * gq + 4, 4 * q : 4 * q + 4, :]
                 if SCALES_ON_GPSIMD:

@@ -10,7 +10,6 @@ I32 = mybir.dt.int32
 U32 = mybir.dt.uint32
 U8 = mybir.dt.uint8
 ALU = mybir.AluOpType
-ACT = mybir.ActivationFunctionType
 
 P = 128
 K = 8192
@@ -18,29 +17,35 @@ N = 2560
 GROUPS = K // 512
 NT = 512
 TILES = N // NT
+MAIN_TILES = TILES - 1
+MAIN = MAIN_TILES * NT
+HALF = NT // 2
 EPS = 1e-5
 FLOPS = 2 * P * K * N
 
-SCALES_ON_GPSIMD = True
-TAIL_GROUPS = 3
 W_BUFS = 8
 X_CHUNKS = 2
+LAST_CHUNKS = (8, 4, 3)
 
 
 def tile_modelnew_w_kernel(
     tc, x, y, weight_words, weight_scales, bias, running_mean, running_var, norm_weight, norm_bias, out
 ):
     nc = tc.nc
-    head_groups = GROUPS - TAIL_GROUPS
     ww = weight_words.rearrange("g p n t -> g p (n t)").bitcast(I32)
 
     with ExitStack() as ctx:
         keep = ctx.enter_context(tc.tile_pool(name="keep", bufs=1))
         wpool = ctx.enter_context(tc.tile_pool(name="wstream", bufs=W_BUFS))
-        opool = ctx.enter_context(tc.tile_pool(name="outs", bufs=5))
-        accp = ctx.enter_context(tc.psum_pool(name="accp", bufs=1))
-        tpp = ctx.enter_context(tc.psum_pool(name="tpp", bufs=3))
+        psum = ctx.enter_context(tc.psum_pool(name="psum", bufs=1))
         ctx.enter_context(tc.manual_schedule())
+
+        turn = [0]
+
+        def work_bank(shape, name):
+            tag = "k%d" % (4 + turn[0] % 4)
+            turn[0] += 1
+            return psum.tile(shape, F32, name=name, tag=tag)
 
         x_sb = []
         xw = K // X_CHUNKS
@@ -67,23 +72,37 @@ def tile_modelnew_w_kernel(
             for q in range(4):
                 dst = planes[gq][32 * q : 32 * q + 16, :]
                 src = weight_scales[4 * gq : 4 * gq + 4, 4 * q : 4 * q + 4, :]
-                if SCALES_ON_GPSIMD:
-                    nc.gpsimd.dma_start(out=dst.bitcast(F32), in_=src.bitcast(F32))
-                else:
-                    nc.sync.dma_start(out=dst.bitcast(I32), in_=src.bitcast(I32))
+                nc.gpsimd.dma_start(out=dst.bitcast(F32), in_=src.bitcast(F32))
 
         w_sb = {}
 
-        def load_w(g):
-            wt = wpool.tile([P, N], U32, name="w", tag="w", align_bytes=64)
-            nc.sync.dma_start(out=wt[:].bitcast(I32), in_=ww[g])
+        def load_main(g):
+            wt = wpool.tile([P, MAIN], U32, name="w", tag="w", align_bytes=64)
+            nc.sync.dma_start(out=wt[:].bitcast(I32), in_=ww[g, :, 0:MAIN])
             w_sb[g] = wt
 
         y_sb = keep.tile([P, N], BF16, name="y_sb")
-        load_w(0)
+        load_main(0)
         nc.sync.dma_start(out=y_sb[:], in_=y)
         for g in range(1, W_BUFS):
-            load_w(g)
+            load_main(g)
+
+        last_w = {}
+
+        def load_last():
+            g0 = 0
+            for count in LAST_CHUNKS:
+                wt = keep.tile([P, count, NT], U32, name="wl%d" % g0, align_bytes=64)
+                nc.sync.dma_start(out=wt[:].bitcast(I32), in_=ww[g0 : g0 + count, :, MAIN:N].rearrange("g p n -> p g n"))
+                for i in range(count):
+                    for h in range(2):
+                        last_w[(g0 + i, h)] = wt[:, i, HALF * h : HALF * (h + 1)]
+                g0 += count
+            assert g0 == GROUPS - 1
+            for h in range(2):
+                wt = keep.tile([P, HALF], U32, name="wh%d" % h, align_bytes=64)
+                nc.sync.dma_start(out=wt[:].bitcast(I32), in_=ww[g0, :, MAIN + HALF * h : MAIN + HALF * (h + 1)])
+                last_w[(g0, h)] = wt[:]
 
         xc = []
         xs = []
@@ -99,7 +118,7 @@ def tile_modelnew_w_kernel(
         for rd in range(8):
             per = 8 // X_CHUNKS
             x32 = x_sb[rd // per][:].bitcast(F32)
-            tp = tpp.tile([P, 2, 2, P], F32, name="tp", tag="tp")
+            tp = work_bank([P, 2, 2, P], "tp")
             for g2 in range(2):
                 base = 256 * ((2 * rd + g2) % (2 * per))
                 for u in range(2):
@@ -115,10 +134,10 @@ def tile_modelnew_w_kernel(
 
         vecs32 = keep.tile([P, P], F32, name="vecs32")
         nc.vector.tensor_copy(out=vecs32[:], in_=vecs[:])
-        tv = tpp.tile([P, 2, 2, P], F32, name="tv", tag="tp")
-        nc.tensor.transpose(tv[:, 0, 0, :], vecs32[:], ident[:])
+        tv = work_bank([P, P], "tv")
+        nc.tensor.transpose(tv[:], vecs32[:], ident[:])
         vt = keep.tile([P, P], F32, name="vt")
-        nc.vector.tensor_copy(out=vt[:], in_=tv[:, 0, 0, :])
+        nc.vector.tensor_copy(out=vt[:], in_=tv[:])
         ab = keep.tile([P, 40], F32, name="ab")
         tmp = keep.tile([P, 40], F32, name="tmp")
         nc.vector.tensor_scalar_add(out=tmp[:, 0:20], in0=vt[:, 40:60], scalar1=EPS)
@@ -134,8 +153,8 @@ def tile_modelnew_w_kernel(
 
         def spread(t):
             cols = slice(NT * t, NT * (t + 1))
-            ba = tpp.tile([P, 4, P], F32, name="ba", tag="tp")
-            bb = tpp.tile([P, 4, P], F32, name="bb", tag="tp")
+            ba = work_bank([P, 4, P], "ba")
+            bb = work_bank([P, 4, P], "bb")
             for i in range(4):
                 c = 4 * t + i
                 nc.tensor.transpose(ba[:, i, :], ab[:, c : c + 1].to_broadcast([P, P]), ident[:])
@@ -150,61 +169,47 @@ def tile_modelnew_w_kernel(
             pm.append(pt)
             qm.append(qt)
 
-        acc = [accp.tile([P, NT], F32, name="acc%d" % j) for j in range(TILES)]
-
-        def mx_pass(g, j, words):
+        def mx_pass(g, acc_ap, words, col0, width):
             rd, g2 = divmod(g, 2)
             gq, kq = divmod(g, 4)
             nc.tensor.matmul_mx(
-                out=acc[j][:],
+                out=acc_ap,
                 lhsT=xc[rd][:, P * g2 : P * (g2 + 1)].bitcast(FP8X4),
                 lhsT_scale=xs[rd][:, P * g2 : P * (g2 + 1)],
                 rhs=words.bitcast(FP8X4),
-                rhs_scale=planes[gq][4 * kq : P, NT * j : NT * (j + 1)],
+                rhs_scale=planes[gq][4 * kq : P, col0 : col0 + width],
                 start=(g == 0),
                 stop=(g == GROUPS - 1),
             )
 
-        tail_w = {}
-
-        def load_tail():
-            for j in range(TILES):
-                cols = slice(NT * j, NT * (j + 1))
-                if j == 0:
-                    wt = keep.tile([P, TAIL_GROUPS, 2 * NT], U32, name="wt01", align_bytes=64)
-                    nc.sync.dma_start(out=wt[:].bitcast(I32), in_=ww[head_groups:GROUPS, :, 0 : 2 * NT].rearrange("g p n -> p g n"))
-                    for i in range(TAIL_GROUPS):
-                        tail_w[(head_groups + i, 0)] = wt[:, i, 0:NT]
-                        tail_w[(head_groups + i, 1)] = wt[:, i, NT : 2 * NT]
-                elif j == 1:
-                    continue
-                elif j < TILES - 1:
-                    wt = keep.tile([P, TAIL_GROUPS, NT], U32, name="wt%d" % j, align_bytes=64)
-                    nc.sync.dma_start(out=wt[:].bitcast(I32), in_=ww[head_groups:GROUPS, :, cols].rearrange("g p n -> p g n"))
-                    for i in range(TAIL_GROUPS):
-                        tail_w[(head_groups + i, j)] = wt[:, i, :]
-                else:
-                    for i in range(TAIL_GROUPS):
-                        wl = keep.tile([P, NT], U32, name="wl%d" % i, align_bytes=64)
-                        nc.sync.dma_start(out=wl[:].bitcast(I32), in_=ww[head_groups + i, :, cols])
-                        tail_w[(head_groups + i, j)] = wl[:]
-
-        for g in range(head_groups):
-            for j in range(TILES):
-                mx_pass(g, j, w_sb[g][:, NT * j : NT * (j + 1)])
+        acc = [psum.tile([P, NT], F32, name="acc%d" % j, tag="k%d" % j) for j in range(MAIN_TILES)]
+        for g in range(GROUPS):
+            for j in range(MAIN_TILES):
+                mx_pass(g, acc[j][:], w_sb[g][:, NT * j : NT * (j + 1)], NT * j, NT)
             nxt = g + W_BUFS
-            if nxt < head_groups:
-                load_w(nxt)
-            elif nxt == head_groups:
-                load_tail()
+            if nxt < GROUPS:
+                load_main(nxt)
+            if nxt == GROUPS - 1:
+                load_last()
             if 1 <= g <= TILES:
                 spread(g - 1)
 
-        for j in range(TILES):
+        for j in range(MAIN_TILES):
             cols = slice(NT * j, NT * (j + 1))
-            for g in range(head_groups, GROUPS):
-                mx_pass(g, j, tail_w[(g, j)])
-            o = opool.tile([P, NT], F32, name="o", tag="o")
+            o = keep.tile([P, NT], F32, name="o%d" % j)
             nc.vector.tensor_tensor(out=o[:], in0=acc[j][:], in1=pm[j][:], op=ALU.mult)
             nc.vector.tensor_tensor(out=o[:], in0=o[:], in1=qm[j][:], op=ALU.add)
             nc.sync.dma_start(out=out[:, cols], in_=o[:])
+
+        half_acc = [psum.tile([P, HALF], F32, name="acch%d" % h, tag="k%d" % (4 + h)) for h in range(2)]
+        for g in range(GROUPS):
+            for h in range(2):
+                mx_pass(g, half_acc[h][:], last_w[(g, h)], MAIN + HALF * h, HALF)
+        o = keep.tile([P, NT], F32, name="o4")
+        for h in range(2):
+            hc = slice(HALF * h, HALF * (h + 1))
+            nc.vector.tensor_tensor(out=o[:, hc], in0=half_acc[h][:], in1=pm[MAIN_TILES][:, hc], op=ALU.mult)
+        for h in range(2):
+            hc = slice(HALF * h, HALF * (h + 1))
+            nc.vector.tensor_tensor(out=o[:, hc], in0=o[:, hc], in1=qm[MAIN_TILES][:, hc], op=ALU.add)
+            nc.sync.dma_start(out=out[:, MAIN + HALF * h : MAIN + HALF * (h + 1)], in_=o[:, hc])

@@ -25,7 +25,8 @@ FLOPS = 2 * P * K * N
 
 W_BUFS = 8
 X_CHUNKS = 2
-LAST_CHUNKS = (8, 4, 3)
+FULL_GROUPS = 7
+LAST_CHUNKS = (4, 3, 1)
 
 
 def tile_modelnew_w_kernel(
@@ -41,9 +42,10 @@ def tile_modelnew_w_kernel(
         ctx.enter_context(tc.manual_schedule())
 
         turn = [0]
+        work_tags = ["k4", "k5", "k6", "k7"]
 
         def work_bank(shape, name):
-            tag = "k%d" % (4 + turn[0] % 4)
+            tag = work_tags[turn[0] % len(work_tags)]
             turn[0] += 1
             return psum.tile(shape, F32, name=name, tag=tag)
 
@@ -75,11 +77,16 @@ def tile_modelnew_w_kernel(
                 nc.gpsimd.dma_start(out=dst.bitcast(F32), in_=src.bitcast(F32))
 
         w_sb = {}
+        last_w = {}
 
         def load_main(g):
-            wt = wpool.tile([P, MAIN], U32, name="w", tag="w", align_bytes=64)
-            nc.sync.dma_start(out=wt[:].bitcast(I32), in_=ww[g, :, 0:MAIN])
+            width = N if g < FULL_GROUPS else MAIN
+            wt = wpool.tile([P, width], U32, name="w", tag="w", align_bytes=64)
+            nc.sync.dma_start(out=wt[:].bitcast(I32), in_=ww[g, :, 0:width])
             w_sb[g] = wt
+            if g < FULL_GROUPS:
+                for h in range(2):
+                    last_w[(g, h)] = wt[:, MAIN + HALF * h : MAIN + HALF * (h + 1)]
 
         y_sb = keep.tile([P, N], BF16, name="y_sb")
         load_main(0)
@@ -87,10 +94,8 @@ def tile_modelnew_w_kernel(
         for g in range(1, W_BUFS):
             load_main(g)
 
-        last_w = {}
-
         def load_last():
-            g0 = 0
+            g0 = FULL_GROUPS
             for count in LAST_CHUNKS:
                 wt = keep.tile([P, count, NT], U32, name="wl%d" % g0, align_bytes=64)
                 nc.sync.dma_start(out=wt[:].bitcast(I32), in_=ww[g0 : g0 + count, :, MAIN:N].rearrange("g p n -> p g n"))
@@ -132,6 +137,8 @@ def tile_modelnew_w_kernel(
                 quantise(rd - 1)
         quantise(7)
 
+        work_tags.remove("k4")
+        work_tags.remove("k5")
         vecs32 = keep.tile([P, P], F32, name="vecs32")
         nc.vector.tensor_copy(out=vecs32[:], in_=vecs[:])
         tv = work_bank([P, P], "tv")
@@ -183,9 +190,13 @@ def tile_modelnew_w_kernel(
             )
 
         acc = [psum.tile([P, NT], F32, name="acc%d" % j, tag="k%d" % j) for j in range(MAIN_TILES)]
+        half_acc = [psum.tile([P, HALF], F32, name="acch%d" % h, tag="k%d" % (4 + h)) for h in range(2)]
         for g in range(GROUPS):
             for j in range(MAIN_TILES):
                 mx_pass(g, acc[j][:], w_sb[g][:, NT * j : NT * (j + 1)], NT * j, NT)
+            if g < FULL_GROUPS:
+                for h in range(2):
+                    mx_pass(g, half_acc[h][:], last_w[(g, h)], MAIN + HALF * h, HALF)
             nxt = g + W_BUFS
             if nxt < GROUPS:
                 load_main(nxt)
@@ -201,8 +212,7 @@ def tile_modelnew_w_kernel(
             nc.vector.tensor_tensor(out=o[:], in0=o[:], in1=qm[j][:], op=ALU.add)
             nc.sync.dma_start(out=out[:, cols], in_=o[:])
 
-        half_acc = [psum.tile([P, HALF], F32, name="acch%d" % h, tag="k%d" % (4 + h)) for h in range(2)]
-        for g in range(GROUPS):
+        for g in range(FULL_GROUPS, GROUPS):
             for h in range(2):
                 mx_pass(g, half_acc[h][:], last_w[(g, h)], MAIN + HALF * h, HALF)
         o = keep.tile([P, NT], F32, name="o4")

from contextlib import ExitStack

import concourse.mybir as mybir
from concourse.masks import make_identity

FP8X4 = mybir.dt.float8_e4m3fn_x4
BF16 = mybir.dt.bfloat16
F32 = mybir.dt.float32
I32 = mybir.dt.int32
U32 = mybir.dt.uint32
U8 = mybir.dt.uint8
ALU = mybir.AluOpType

P = 128
K = 8192
N = 2560
GROUPS = K // 512
NT = 512
TILES = N // NT
MAIN_TILES = TILES - 1
MAIN = MAIN_TILES * NT
HALF = NT // 2
EPS = 1e-5
FLOPS = 2 * P * K * N

W_BUFS = 8
X_CHUNKS = 2
FULL_GROUPS = 7
LAST_CHUNKS = (4, 3, 1)


def tile_modelnew_w_kernel(
    tc, x, y, weight_words, weight_scales, bias, running_mean, running_var, norm_weight, norm_bias, out
):
    nc = tc.nc
    ww = weight_words.rearrange("g p n t -> g p (n t)").bitcast(I32)

    with ExitStack() as ctx:
        keep = ctx.enter_context(tc.tile_pool(name="keep", bufs=1))
        wpool = ctx.enter_context(tc.tile_pool(name="wstream", bufs=W_BUFS))
        psum = ctx.enter_context(tc.psum_pool(name="psum", bufs=1))
        ctx.enter_context(tc.manual_schedule())

        turn = [0]
        work_tags = ["k4", "k5", "k6", "k7"]

        def work_bank(shape, name):
            tag = work_tags[turn[0] % len(work_tags)]
            turn[0] += 1
            return psum.tile(shape, F32, name=name, tag=tag)

        x_sb = []
        xw = K // X_CHUNKS
        for c in range(X_CHUNKS):
            xt = keep.tile([P, xw], BF16, name="x%d" % c)
            nc.sync.dma_start(out=xt[:], in_=x[:, xw * c : xw * (c + 1)])
            x_sb.append(xt)

        ident = keep.tile([P, P], F32, name="ident")
        make_identity(nc, ident[:])

        planes = []
        for gq in range(4):
            pl = keep.tile([P, N], U8, name="pl%d" % gq, align_bytes=64)
            nc.vector.memset(pl[:].bitcast(I32), 0)
            planes.append(pl)
        vecs = keep.tile([P, P], BF16, name="vecs")
        nc.vector.memset(vecs[:], 0.0)

        for v, vec_ap in enumerate((bias, running_mean, running_var, norm_weight, norm_bias)):
            nc.scalar.dma_start(out=vecs[20 * v : 20 * v + 20, :], in_=vec_ap.rearrange("(c j) -> c j", j=P))

        for gq in range(4):
            for q in range(4):
                dst = planes[gq][32 * q : 32 * q + 16, :]
                src = weight_scales[4 * gq : 4 * gq + 4, 4 * q : 4 * q + 4, :]
                nc.gpsimd.dma_start(out=dst.bitcast(F32), in_=src.bitcast(F32))

        w_sb = {}
        last_w = {}

        def load_main(g):
            width = N if g < FULL_GROUPS else MAIN
            wt = wpool.tile([P, width], U32, name="w", tag="w", align_bytes=64)
            nc.sync.dma_start(out=wt[:].bitcast(I32), in_=ww[g, :, 0:width])
            w_sb[g] = wt
            if g < FULL_GROUPS:
                for h in range(2):
                    last_w[(g, h)] = wt[:, MAIN + HALF * h : MAIN + HALF * (h + 1)]

        y_sb = keep.tile([P, N], BF16, name="y_sb")
        load_main(0)
        nc.sync.dma_start(out=y_sb[:], in_=y)
        for g in range(1, W_BUFS):
            load_main(g)

        def load_last():
            g0 = FULL_GROUPS
            for count in LAST_CHUNKS:
                wt = keep.tile([P, count, NT], U32, name="wl%d" % g0, align_bytes=64)
                nc.sync.dma_start(out=wt[:].bitcast(I32), in_=ww[g0 : g0 + count, :, MAIN:N].rearrange("g p n -> p g n"))
                for i in range(count):
                    for h in range(2):
                        last_w[(g0 + i, h)] = wt[:, i, HALF * h : HALF * (h + 1)]
                g0 += count
            assert g0 == GROUPS - 1
            for h in range(2):
                wt = keep.tile([P, HALF], U32, name="wh%d" % h, align_bytes=64)
                nc.sync.dma_start(out=wt[:].bitcast(I32), in_=ww[g0, :, MAIN + HALF * h : MAIN + HALF * (h + 1)])
                last_w[(g0, h)] = wt[:]

        xc = []
        xs = []
        grps = []

        def quantise(rd):
            nc.vector.quantize_mx(
                out=xc[rd][:].bitcast(FP8X4),
                scales=xs[rd][:],
                in_=grps[rd][:].rearrange("p g b t -> p (g b t)"),
            )

        for rd in range(8):
            per = 8 // X_CHUNKS
            x32 = x_sb[rd // per][:].bitcast(F32)
            tp = work_bank([P, 2, 2, P], "tp")
            for g2 in range(2):
                base = 256 * ((2 * rd + g2) % (2 * per))
                for u in range(2):
                    nc.tensor.transpose(tp[:, g2, u, :], x32[:, base + u : base + 256 : 2], ident[:])
            grp = keep.tile([P, 2, P, 4], BF16, name="grp%d" % rd, align_bytes=64)
            nc.scalar.copy(out=grp[:].bitcast(F32), in_=tp[:].rearrange("p g u b -> p g b u"))
            grps.append(grp)
            xc.append(keep.tile([P, 2 * P], U32, name="xc%d" % rd, align_bytes=64))
            xs.append(keep.tile([P, 2 * P], U8, name="xs%d" % rd, align_bytes=64))
            if rd >= 1:
                quantise(rd - 1)
        quantise(7)

        work_tags.remove("k4")
        work_tags.remove("k5")
        vecs32 = keep.tile([P, P], F32, name="vecs32")
        nc.vector.tensor_copy(out=vecs32[:], in_=vecs[:])
        tv = work_bank([P, P], "tv")
        nc.tensor.transpose(tv[:], vecs32[:], ident[:])
        vt = keep.tile([P, P], F32, name="vt")
        nc.vector.tensor_copy(out=vt[:], in_=tv[:])
        ab = keep.tile([P, 40], F32, name="ab")
        tmp = keep.tile([P, 40], F32, name="tmp")
        nc.vector.tensor_scalar_add(out=tmp[:, 0:20], in0=vt[:, 40:60], scalar1=EPS)
        nc.scalar.sqrt(out=tmp[:, 0:20], in_=tmp[:, 0:20])
        nc.vector.reciprocal(out=tmp[:, 0:20], in_=tmp[:, 0:20])
        nc.vector.tensor_tensor(out=ab[:, 0:20], in0=tmp[:, 0:20], in1=vt[:, 60:80], op=ALU.mult)
        nc.vector.tensor_tensor(out=tmp[:, 20:40], in0=vt[:, 0:20], in1=vt[:, 20:40], op=ALU.subtract)
        nc.vector.tensor_tensor(out=tmp[:, 20:40], in0=tmp[:, 20:40], in1=ab[:, 0:20], op=ALU.mult)
        nc.vector.tensor_tensor(out=ab[:, 20:40], in0=tmp[:, 20:40], in1=vt[:, 80:100], op=ALU.add)

        pm = []
        qm = []

        def spread(t):
            cols = slice(NT * t, NT * (t + 1))
            ba = work_bank([P, 4, P], "ba")
            bb = work_bank([P, 4, P], "bb")
            for i in range(4):
                c = 4 * t + i
                nc.tensor.transpose(ba[:, i, :], ab[:, c : c + 1].to_broadcast([P, P]), ident[:])
            for i in range(4):
                c = 20 + 4 * t + i
                nc.tensor.transpose(bb[:, i, :], ab[:, c : c + 1].to_broadcast([P, P]), ident[:])
            pt = keep.tile([P, NT], F32, name="pm%d" % t)
            qt = keep.tile([P, NT], F32, name="qm%d" % t)
            nc.vector.tensor_tensor(out=pt[:], in0=ba[:].rearrange("p i j -> p (i j)"), in1=y_sb[:, cols], op=ALU.mult)
            nc.vector.tensor_tensor(out=qt[:], in0=bb[:].rearrange("p i j -> p (i j)"), in1=y_sb[:, cols], op=ALU.add)
            nc.vector.tensor_tensor(out=qt[:], in0=qt[:], in1=y_sb[:, cols], op=ALU.mult)
            pm.append(pt)
            qm.append(qt)

        def mx_pass(g, acc_ap, words, col0, width):
            rd, g2 = divmod(g, 2)
            gq, kq = divmod(g, 4)
            nc.tensor.matmul_mx(
                out=acc_ap,
                lhsT=xc[rd][:, P * g2 : P * (g2 + 1)].bitcast(FP8X4),
                lhsT_scale=xs[rd][:, P * g2 : P * (g2 + 1)],
                rhs=words.bitcast(FP8X4),
                rhs_scale=planes[gq][4 * kq : P, col0 : col0 + width],
                start=(g == 0),
                stop=(g == GROUPS - 1),
            )

        acc = [psum.tile([P, NT], F32, name="acc%d" % j, tag="k%d" % j) for j in range(MAIN_TILES)]
        half_acc = [psum.tile([P, HALF], F32, name="acch%d" % h, tag="k%d" % (4 + h)) for h in range(2)]
        for g in range(GROUPS):
            for j in range(MAIN_TILES):
                mx_pass(g, acc[j][:], w_sb[g][:, NT * j : NT * (j + 1)], NT * j, NT)
            if g < FULL_GROUPS:
                for h in range(2):
                    mx_pass(g, half_acc[h][:], last_w[(g, h)], MAIN + HALF * h, HALF)
            nxt = g + W_BUFS
            if nxt < GROUPS:
                load_main(nxt)
            if nxt == GROUPS - 1:
                load_last()
            if 1 <= g <= TILES:
                spread(g - 1)

        for j in range(MAIN_TILES):
            cols = slice(NT * j, NT * (j + 1))
            o = keep.tile([P, NT], F32, name="o%d" % j)
            nc.vector.tensor_tensor(out=o[:], in0=acc[j][:], in1=pm[j][:], op=ALU.mult)
            nc.vector.tensor_tensor(out=o[:], in0=o[:], in1=qm[j][:], op=ALU.add)
            nc.sync.dma_start(out=out[:, cols], in_=o[:])

        for g in range(FULL_GROUPS, GROUPS):
            for h in range(2):
                mx_pass(g, half_acc[h][:], last_w[(g, h)], MAIN + HALF * h, HALF)
        o = keep.tile([P, NT], F32, name="o4")
        for h in range(2):
            hc = slice(HALF * h, HALF * (h + 1))
            nc.vector.tensor_tensor(out=o[:, hc], in0=half_acc[h][:], in1=pm[MAIN_TILES][:, hc], op=ALU.mult)
        for h in range(2):
            hc = slice(HALF * h, HALF * (h + 1))
            nc.vector.tensor_tensor(out=o[:, hc], in0=o[:, hc], in1=qm[MAIN_TILES][:, hc], op=ALU.add)
            nc.sync.dma_start(out=out[:, MAIN + HALF * h : MAIN + HALF * (h + 1)], in_=o[:, hc])
